import numpy as np
import ml_dtypes

BF16 = ml_dtypes.bfloat16


def bf(x):
    return np.asarray(x, np.float32).astype(BF16)


def f32(x):
    return np.asarray(x, np.float32)


def f64(x):
    return np.asarray(x).astype(np.float64)


def striped(idx):
    return np.tile(idx.reshape(-1, 16).T, (8, 1))


C, S, N = 512, 512, 256


def setup_inputs():
    sc = 0.5 / np.sqrt(N)
    return {"base": f32(np.random.standard_normal((C, S))), "h": bf(np.random.standard_normal((C, N))), "filt_t": bf(sc * np.random.standard_normal((N, N))), "adj_t": bf(sc * np.random.standard_normal((N, N))), "cw_filt": f32(1.0 + 0.1 * np.random.standard_normal((C, 1))), "cw_id": f32(1.0 + 0.1 * np.random.standard_normal((C, 1))), "cw_adj": f32(1.0 + 0.1 * np.random.standard_normal((C, 1))), "offs": striped(np.random.permutation(S)[:N])}


def reference(base, h, filt_t, adj_t, cw_filt, cw_id, cw_adj, offs):
    idx = offs[:16].T.reshape(-1)
    hh = f64(h)
    pf = hh @ f64(filt_t)
    pa = hh @ f64(adj_t)
    u = f64(cw_filt) * pf + f64(cw_id) * hh
    v = f64(cw_adj) * pa
    res = f64(base).copy()
    res[:, idx] = u + v
    return res

@@ -1,0 +1,80 @@
+import concourse.mybir as mybir
+from concourse.masks import make_identity
+
+P = 128
+C, S, N = 512, 512, 256
+NB = C // P
+NK = N // P
+
+FLOPS = 2 * 2 * C * N * N
+
+BF16, F32, U16 = mybir.dt.bfloat16, mybir.dt.float32, mybir.dt.uint16
+MULT, ADD = mybir.AluOpType.mult, mybir.AluOpType.add
+COPY = mybir.ActivationFunctionType.Copy
+
+
+def tile_eigenvaluesegmentprec_kernel(
+    tc, base, h, filt_t, adj_t, cw_filt, cw_id, cw_adj, offs, out
+):
+    nc = tc.nc
+
+    base_blocks = base.rearrange("(p b) s -> p b s", b=NB)
+    out_blocks = out.rearrange("(p b) s -> p b s", b=NB)
+
+    with (
+        tc.tile_pool(name="held", bufs=1) as held,
+        tc.tile_pool(name="work", bufs=NB) as work,
+        tc.psum_pool(name="flip", bufs=NB) as flip,
+        tc.psum_pool(name="prod", bufs=NB) as prod,
+    ):
+        offsets = held.tile([P, N // 16], U16, name="offsets")
+        nc.sync.dma_start(offsets[:], offs)
+
+        h_rows = held.tile([P, NB, N], BF16, name="h_rows")
+        nc.sync.dma_start(h_rows[:], h.rearrange("(p b) i -> p b i", b=NB))
+
+        bases = held.tile([P, NK, 2 * N], BF16, name="bases")
+        nc.scalar.dma_start(bases[:, :, 0:N], filt_t.rearrange("(k p) j -> p k j", p=P))
+        nc.scalar.dma_start(bases[:, :, N : 2 * N], adj_t.rearrange("(k p) j -> p k j", p=P))
+
+        w_filt = held.tile([P, NB], F32, name="w_filt")
+        w_id = held.tile([P, NB], F32, name="w_id")
+        w_adj = held.tile([P, NB], F32, name="w_adj")
+        nc.scalar.dma_start(w_id[:], cw_id.rearrange("(p b) o -> p (b o)", b=NB))
+        nc.scalar.dma_start(w_filt[:], cw_filt.rearrange("(p b) o -> p (b o)", b=NB))
+        nc.scalar.dma_start(w_adj[:], cw_adj.rearrange("(p b) o -> p (b o)", b=NB))
+
+        windows = [held.tile([P, S], F32, name=f"window{b}") for b in range(NB)]
+        for b in range(NB):
+            nc.sync.dma_start(windows[b][:], base_blocks[:, b, :])
+
+        identity = held.tile([P, P], BF16, name="identity")
+        make_identity(nc, identity[:])
+
+        for b in range(NB):
+            h_flip_psum = flip.tile([P, NK, P], BF16, name="h_flip_psum")
+            for k in range(NK):
+                nc.tensor.transpose(
+                    h_flip_psum[:, k, :], h_rows[:, b, k * P : (k + 1) * P], identity[:]
+                )
+            h_flip = work.tile([P, NK, P], BF16, name="h_flip")
+            nc.scalar.copy(h_flip[:], h_flip_psum[:])
+
+            products = prod.tile([P, 2 * N], F32, name="products")
+            for k in range(NK):
+                nc.tensor.matmul(
+                    products[:], h_flip[:, k, :], bases[:, k, :],
+                    start=(k == 0), stop=(k == NK - 1),
+                )
+
+            own = work.tile([P, N], F32, name="own")
+            nc.scalar.activation(own[:], h_rows[:, b, :], COPY, scale=w_id[:, b : b + 1])
+            v = work.tile([P, N], F32, name="v")
+            nc.scalar.activation(v[:], products[:, N : 2 * N], COPY, scale=w_adj[:, b : b + 1])
+            u = work.tile([P, N], F32, name="u")
+            nc.vector.scalar_tensor_tensor(
+                u[:], products[:, 0:N], w_filt[:, b : b + 1], own[:], MULT, ADD
+            )
+
+            nc.vector.tensor_tensor(windows[b][:].indirect(offsets[:]), u[:], v[:], ADD)
+            nc.sync.dma_start(out_blocks[:, b, :], windows[b][:])

@@ -27,15 +27,15 @@ def tile_eigenvaluesegmentprec_kernel(
         tc.psum_pool(name="flip", bufs=NB) as flip,
         tc.psum_pool(name="prod", bufs=NB) as prod,
     ):
-        offsets = held.tile([P, N // 16], U16, name="offsets")
-        nc.sync.dma_start(offsets[:], offs)
-
         h_rows = held.tile([P, NB, N], BF16, name="h_rows")
         nc.sync.dma_start(h_rows[:], h.rearrange("(p b) i -> p b i", b=NB))
 
         bases = held.tile([P, NK, 2 * N], BF16, name="bases")
-        nc.scalar.dma_start(bases[:, :, 0:N], filt_t.rearrange("(k p) j -> p k j", p=P))
-        nc.scalar.dma_start(bases[:, :, N : 2 * N], adj_t.rearrange("(k p) j -> p k j", p=P))
+        nc.sync.dma_start(bases[:, :, 0:N], filt_t.rearrange("(k p) j -> p k j", p=P))
+        nc.sync.dma_start(bases[:, :, N : 2 * N], adj_t.rearrange("(k p) j -> p k j", p=P))
+
+        offsets = held.tile([P, N // 16], U16, name="offsets")
+        nc.sync.dma_start(offsets[:], offs)
 
         w_filt = held.tile([P, NB], F32, name="w_filt")
         w_id = held.tile([P, NB], F32, name="w_id")

@@ -9,7 +9,7 @@ NK = N // P
 FLOPS = 2 * 2 * C * N * N
 
 BF16, F32, U16 = mybir.dt.bfloat16, mybir.dt.float32, mybir.dt.uint16
-MULT, ADD = mybir.AluOpType.mult, mybir.AluOpType.add
+ADD = mybir.AluOpType.add
 COPY = mybir.ActivationFunctionType.Copy
 
 
@@ -68,13 +68,13 @@ def tile_eigenvaluesegmentprec_kernel(
                 )
 
             own = work.tile([P, N], F32, name="own")
-            nc.scalar.activation(own[:], h_rows[:, b, :], COPY, scale=w_id[:, b : b + 1])
+            nc.gpsimd.tensor_scalar_mul(own[:], h_rows[:, b, :], w_id[:, b : b + 1])
+            filtered = work.tile([P, N], F32, name="filtered")
+            nc.scalar.activation(filtered[:], products[:, 0:N], COPY, scale=w_filt[:, b : b + 1])
+            u = work.tile([P, N], F32, name="u")
+            nc.gpsimd.tensor_tensor(u[:], filtered[:], own[:], ADD)
             v = work.tile([P, N], F32, name="v")
             nc.scalar.activation(v[:], products[:, N : 2 * N], COPY, scale=w_adj[:, b : b + 1])
-            u = work.tile([P, N], F32, name="u")
-            nc.vector.scalar_tensor_tensor(
-                u[:], products[:, 0:N], w_filt[:, b : b + 1], own[:], MULT, ADD
-            )
 
             nc.vector.tensor_tensor(windows[b][:].indirect(offsets[:]), u[:], v[:], ADD)
             nc.sync.dma_start(out_blocks[:, b, :], windows[b][:])

@@ -9,7 +9,7 @@ NK = N // P
 FLOPS = 2 * 2 * C * N * N
 
 BF16, F32, U16 = mybir.dt.bfloat16, mybir.dt.float32, mybir.dt.uint16
-ADD = mybir.AluOpType.add
+MULT, ADD = mybir.AluOpType.mult, mybir.AluOpType.add
 COPY = mybir.ActivationFunctionType.Copy
 
 
@@ -51,6 +51,7 @@ def tile_eigenvaluesegmentprec_kernel(
         identity = held.tile([P, P], BF16, name="identity")
         make_identity(nc, identity[:])
 
+        h_flips = []
         for b in range(NB):
             h_flip_psum = flip.tile([P, NK, P], BF16, name="h_flip_psum")
             for k in range(NK):
@@ -58,23 +59,25 @@ def tile_eigenvaluesegmentprec_kernel(
                     h_flip_psum[:, k, :], h_rows[:, b, k * P : (k + 1) * P], identity[:]
                 )
             h_flip = work.tile([P, NK, P], BF16, name="h_flip")
-            nc.scalar.copy(h_flip[:], h_flip_psum[:])
+            nc.vector.tensor_copy(h_flip[:], h_flip_psum[:])
+            h_flips.append(h_flip)
 
+        for b in range(NB):
             products = prod.tile([P, 2 * N], F32, name="products")
             for k in range(NK):
                 nc.tensor.matmul(
-                    products[:], h_flip[:, k, :], bases[:, k, :],
+                    products[:], h_flips[b][:, k, :], bases[:, k, :],
                     start=(k == 0), stop=(k == NK - 1),
                 )
 
             own = work.tile([P, N], F32, name="own")
-            nc.gpsimd.tensor_scalar_mul(own[:], h_rows[:, b, :], w_id[:, b : b + 1])
-            filtered = work.tile([P, N], F32, name="filtered")
-            nc.scalar.activation(filtered[:], products[:, 0:N], COPY, scale=w_filt[:, b : b + 1])
-            u = work.tile([P, N], F32, name="u")
-            nc.gpsimd.tensor_tensor(u[:], filtered[:], own[:], ADD)
+            nc.scalar.activation(own[:], h_rows[:, b, :], COPY, scale=w_id[:, b : b + 1])
             v = work.tile([P, N], F32, name="v")
             nc.scalar.activation(v[:], products[:, N : 2 * N], COPY, scale=w_adj[:, b : b + 1])
+            u = work.tile([P, N], F32, name="u")
+            nc.vector.scalar_tensor_tensor(
+                u[:], products[:, 0:N], w_filt[:, b : b + 1], own[:], MULT, ADD
+            )
 
             nc.vector.tensor_tensor(windows[b][:].indirect(offsets[:]), u[:], v[:], ADD)
             nc.sync.dma_start(out_blocks[:, b, :], windows[b][:])

@@ -6,6 +6,8 @@ C, S, N = 512, 512, 256
 NB = C // P
 NK = N // P
 
+WARM_UP_MATMULS = 12
+
 FLOPS = 2 * 2 * C * N * N
 
 BF16, F32, U16 = mybir.dt.bfloat16, mybir.dt.float32, mybir.dt.uint16
@@ -24,9 +26,19 @@ def tile_eigenvaluesegmentprec_kernel(
     with (
         tc.tile_pool(name="held", bufs=1) as held,
         tc.tile_pool(name="work", bufs=NB) as work,
-        tc.psum_pool(name="flip", bufs=NB) as flip,
+        tc.psum_pool(name="flip", bufs=2) as flip,
         tc.psum_pool(name="prod", bufs=NB) as prod,
+        tc.psum_pool(name="idle", bufs=1) as idle,
     ):
+        zeros = held.tile([P, P], BF16, name="zeros")
+        nc.vector.memset(zeros[:], 0.0)
+        unused = idle.tile([P, P], F32, name="unused")
+        for _ in range(WARM_UP_MATMULS):
+            nc.tensor.matmul(unused[:], zeros[:], zeros[:], start=True, stop=True)
+
+        primed = held.tile([P, 1], F32, name="primed")
+        nc.scalar.activation(primed[:], zeros[:, 0:1], COPY)
+
         h_rows = held.tile([P, NB, N], BF16, name="h_rows")
         nc.sync.dma_start(h_rows[:], h.rearrange("(p b) i -> p b i", b=NB))
 

@@ -6,7 +6,7 @@ C, S, N = 512, 512, 256
 NB = C // P
 NK = N // P
 
-WARM_UP_MATMULS = 12
+WARM_UP_MATMULS = 16
 
 FLOPS = 2 * 2 * C * N * N
 
@@ -31,7 +31,7 @@ def tile_eigenvaluesegmentprec_kernel(
         tc.psum_pool(name="idle", bufs=1) as idle,
     ):
         zeros = held.tile([P, P], BF16, name="zeros")
-        nc.vector.memset(zeros[:], 0.0)
+        nc.gpsimd.memset(zeros[:], 0.0)
         unused = idle.tile([P, P], F32, name="unused")
         for _ in range(WARM_UP_MATMULS):
             nc.tensor.matmul(unused[:], zeros[:], zeros[:], start=True, stop=True)

@@ -20,6 +20,7 @@ def tile_eigenvaluesegmentprec_kernel(
 ):
     nc = tc.nc
 
+    h_blocks = h.rearrange("(p b) i -> p b i", b=NB)
     base_blocks = base.rearrange("(p b) s -> p b s", b=NB)
     out_blocks = out.rearrange("(p b) s -> p b s", b=NB)
 
@@ -27,7 +28,7 @@ def tile_eigenvaluesegmentprec_kernel(
         tc.tile_pool(name="held", bufs=1) as held,
         tc.tile_pool(name="work", bufs=NB) as work,
         tc.psum_pool(name="flip", bufs=2) as flip,
-        tc.psum_pool(name="prod", bufs=NB) as prod,
+        tc.psum_pool(name="prod", bufs=2) as prod,
         tc.psum_pool(name="idle", bufs=1) as idle,
     ):
         zeros = held.tile([P, P], BF16, name="zeros")
@@ -39,57 +40,73 @@ def tile_eigenvaluesegmentprec_kernel(
         primed = held.tile([P, 1], F32, name="primed")
         nc.scalar.activation(primed[:], zeros[:, 0:1], COPY)
 
+        identity = held.tile([P, P], BF16, name="identity")
+        make_identity(nc, identity[:])
+
         h_rows = held.tile([P, NB, N], BF16, name="h_rows")
-        nc.sync.dma_start(h_rows[:], h.rearrange("(p b) i -> p b i", b=NB))
+        nc.sync.dma_start(h_rows[:], h_blocks)
 
-        bases = held.tile([P, NK, 2 * N], BF16, name="bases")
-        nc.sync.dma_start(bases[:, :, 0:N], filt_t.rearrange("(k p) j -> p k j", p=P))
-        nc.sync.dma_start(bases[:, :, N : 2 * N], adj_t.rearrange("(k p) j -> p k j", p=P))
-
-        offsets = held.tile([P, N // 16], U16, name="offsets")
-        nc.sync.dma_start(offsets[:], offs)
+        adj = held.tile([P, NK, N], BF16, name="adj")
+        nc.sync.dma_start(adj[:], adj_t.rearrange("(k p) j -> p k j", p=P))
+        filt = held.tile([P, NK, N], BF16, name="filt")
+        nc.sync.dma_start(filt[:], filt_t.rearrange("(k p) j -> p k j", p=P))
 
         w_filt = held.tile([P, NB], F32, name="w_filt")
         w_id = held.tile([P, NB], F32, name="w_id")
         w_adj = held.tile([P, NB], F32, name="w_adj")
-        nc.scalar.dma_start(w_id[:], cw_id.rearrange("(p b) o -> p (b o)", b=NB))
-        nc.scalar.dma_start(w_filt[:], cw_filt.rearrange("(p b) o -> p (b o)", b=NB))
-        nc.scalar.dma_start(w_adj[:], cw_adj.rearrange("(p b) o -> p (b o)", b=NB))
+        nc.sync.dma_start(w_id[:], cw_id.rearrange("(p b) o -> p (b o)", b=NB))
+        nc.sync.dma_start(w_filt[:], cw_filt.rearrange("(p b) o -> p (b o)", b=NB))
+        nc.sync.dma_start(w_adj[:], cw_adj.rearrange("(p b) o -> p (b o)", b=NB))
+
+        offsets = held.tile([P, N // 16], U16, name="offsets")
+        nc.sync.dma_start(offsets[:], offs)
 
         windows = [held.tile([P, S], F32, name=f"window{b}") for b in range(NB)]
         for b in range(NB):
             nc.sync.dma_start(windows[b][:], base_blocks[:, b, :])
 
-        identity = held.tile([P, P], BF16, name="identity")
-        make_identity(nc, identity[:])
-
-        h_flips = []
-        for b in range(NB):
+        def flipped(b, copy_out_of_psum):
             h_flip_psum = flip.tile([P, NK, P], BF16, name="h_flip_psum")
             for k in range(NK):
                 nc.tensor.transpose(
                     h_flip_psum[:, k, :], h_rows[:, b, k * P : (k + 1) * P], identity[:]
                 )
             h_flip = work.tile([P, NK, P], BF16, name="h_flip")
-            nc.vector.tensor_copy(h_flip[:], h_flip_psum[:])
-            h_flips.append(h_flip)
+            copy_out_of_psum(h_flip[:], h_flip_psum[:])
+            return h_flip
 
-        for b in range(NB):
-            products = prod.tile([P, 2 * N], F32, name="products")
+        def product(h_flip, basis, name):
+            h_basis = prod.tile([P, N], F32, name=name)
             for k in range(NK):
                 nc.tensor.matmul(
-                    products[:], h_flips[b][:, k, :], bases[:, k, :],
+                    h_basis[:], h_flip[:, k, :], basis[:, k, :],
                     start=(k == 0), stop=(k == NK - 1),
                 )
+            return h_basis
 
+        def terms(b, h_flip):
+            h_adj = product(h_flip, adj, "h_adj")
+            h_filt = product(h_flip, filt, "h_filt")
             own = work.tile([P, N], F32, name="own")
             nc.scalar.activation(own[:], h_rows[:, b, :], COPY, scale=w_id[:, b : b + 1])
             v = work.tile([P, N], F32, name="v")
-            nc.scalar.activation(v[:], products[:, N : 2 * N], COPY, scale=w_adj[:, b : b + 1])
+            nc.scalar.activation(v[:], h_adj[:], COPY, scale=w_adj[:, b : b + 1])
             u = work.tile([P, N], F32, name="u")
             nc.vector.scalar_tensor_tensor(
-                u[:], products[:, 0:N], w_filt[:, b : b + 1], own[:], MULT, ADD
+                u[:], h_filt[:], w_filt[:, b : b + 1], own[:], MULT, ADD
             )
+            return u, v
 
+        def place(b, u, v):
             nc.vector.tensor_tensor(windows[b][:].indirect(offsets[:]), u[:], v[:], ADD)
             nc.sync.dma_start(out_blocks[:, b, :], windows[b][:])
+
+        h_flips = [flipped(b, nc.vector.tensor_copy) for b in (0, 1)]
+        sums = [terms(0, h_flips[0])]
+        place(0, *sums[0])
+        sums.append(terms(1, h_flips[1]))
+        h_flips += [flipped(b, nc.scalar.copy) for b in (2, 3)]
+        for b in range(1, NB):
+            if b + 1 < NB:
+                sums.append(terms(b + 1, h_flips[b + 1]))
+            place(b, *sums[b])

@@ -6,7 +6,10 @@ C, S, N = 512, 512, 256
 NB = C // P
 NK = N // P
 
+PSUM_BANKS = 8
+
 WARM_UP_MATMULS = 16
+BY_VECTOR = 2
 
 FLOPS = 2 * 2 * C * N * N
 
@@ -27,9 +30,8 @@ def tile_eigenvaluesegmentprec_kernel(
     with (
         tc.tile_pool(name="held", bufs=1) as held,
         tc.tile_pool(name="work", bufs=NB) as work,
-        tc.psum_pool(name="flip", bufs=2) as flip,
-        tc.psum_pool(name="prod", bufs=2) as prod,
         tc.psum_pool(name="idle", bufs=1) as idle,
+        tc.psum_pool(name="psum", bufs=PSUM_BANKS - 1) as psum,
     ):
         zeros = held.tile([P, P], BF16, name="zeros")
         nc.gpsimd.memset(zeros[:], 0.0)
@@ -42,9 +44,13 @@ def tile_eigenvaluesegmentprec_kernel(
 
         identity = held.tile([P, P], BF16, name="identity")
         make_identity(nc, identity[:])
+        identity_f32 = held.tile([P, P], F32, name="identity_f32")
+        make_identity(nc, identity_f32[:])
 
         h_rows = held.tile([P, NB, N], BF16, name="h_rows")
         nc.sync.dma_start(h_rows[:], h_blocks)
+        w_id = held.tile([P, NB], F32, name="w_id")
+        nc.sync.dma_start(w_id[:], cw_id.rearrange("(p b) o -> p (b o)", b=NB))
 
         adj = held.tile([P, NK, N], BF16, name="adj")
         nc.sync.dma_start(adj[:], adj_t.rearrange("(k p) j -> p k j", p=P))
@@ -52,9 +58,7 @@ def tile_eigenvaluesegmentprec_kernel(
         nc.sync.dma_start(filt[:], filt_t.rearrange("(k p) j -> p k j", p=P))
 
         w_filt = held.tile([P, NB], F32, name="w_filt")
-        w_id = held.tile([P, NB], F32, name="w_id")
         w_adj = held.tile([P, NB], F32, name="w_adj")
-        nc.sync.dma_start(w_id[:], cw_id.rearrange("(p b) o -> p (b o)", b=NB))
         nc.sync.dma_start(w_filt[:], cw_filt.rearrange("(p b) o -> p (b o)", b=NB))
         nc.sync.dma_start(w_adj[:], cw_adj.rearrange("(p b) o -> p (b o)", b=NB))
 
@@ -65,18 +69,23 @@ def tile_eigenvaluesegmentprec_kernel(
         for b in range(NB):
             nc.sync.dma_start(windows[b][:], base_blocks[:, b, :])
 
-        def flipped(b, copy_out_of_psum):
-            h_flip_psum = flip.tile([P, NK, P], BF16, name="h_flip_psum")
+        def flipped(b):
+            h_flip_psum = psum.tile([P, NK, P], BF16, name="h_flip_psum", tag="bank")
             for k in range(NK):
                 nc.tensor.transpose(
                     h_flip_psum[:, k, :], h_rows[:, b, k * P : (k + 1) * P], identity[:]
                 )
             h_flip = work.tile([P, NK, P], BF16, name="h_flip")
-            copy_out_of_psum(h_flip[:], h_flip_psum[:])
+            nc.vector.tensor_copy(h_flip[:], h_flip_psum[:])
             return h_flip
 
+        def own_term(b):
+            own = work.tile([P, N], F32, name="own")
+            nc.scalar.activation(own[:], h_rows[:, b, :], COPY, scale=w_id[:, b : b + 1])
+            return own
+
         def product(h_flip, basis, name):
-            h_basis = prod.tile([P, N], F32, name=name)
+            h_basis = psum.tile([P, N], F32, name=name, tag="bank")
             for k in range(NK):
                 nc.tensor.matmul(
                     h_basis[:], h_flip[:, k, :], basis[:, k, :],
@@ -84,29 +93,40 @@ def tile_eigenvaluesegmentprec_kernel(
                 )
             return h_basis
 
-        def terms(b, h_flip):
-            h_adj = product(h_flip, adj, "h_adj")
-            h_filt = product(h_flip, filt, "h_filt")
-            own = work.tile([P, N], F32, name="own")
-            nc.scalar.activation(own[:], h_rows[:, b, :], COPY, scale=w_id[:, b : b + 1])
-            v = work.tile([P, N], F32, name="v")
-            nc.scalar.activation(v[:], h_adj[:], COPY, scale=w_adj[:, b : b + 1])
-            u = work.tile([P, N], F32, name="u")
-            nc.vector.scalar_tensor_tensor(
-                u[:], h_filt[:], w_filt[:, b : b + 1], own[:], MULT, ADD
-            )
-            return u, v
+        def scaled(h_basis, weights, b, name):
+            term = work.tile([P, N], F32, name=name)
+            nc.scalar.activation(term[:], h_basis[:], COPY, scale=weights[:, b : b + 1])
+            return term
 
         def place(b, u, v):
             nc.vector.tensor_tensor(windows[b][:].indirect(offsets[:]), u[:], v[:], ADD)
             nc.sync.dma_start(out_blocks[:, b, :], windows[b][:])
 
-        h_flips = [flipped(b, nc.vector.tensor_copy) for b in (0, 1)]
-        sums = [terms(0, h_flips[0])]
-        place(0, *sums[0])
-        sums.append(terms(1, h_flips[1]))
-        h_flips += [flipped(b, nc.scalar.copy) for b in (2, 3)]
-        for b in range(1, NB):
-            if b + 1 < NB:
-                sums.append(terms(b + 1, h_flips[b + 1]))
-            place(b, *sums[b])
+        h_flips = [flipped(b) for b in range(NB)]
+        owns = [own_term(b) for b in range(NB)]
+
+        h_adjs, h_filts = [], []
+        for b in range(NB):
+            h_adjs.append(product(h_flips[b], adj, "h_adj"))
+            h_filts.append(product(h_flips[b], filt, "h_filt"))
+
+        for b in range(BY_VECTOR):
+            v = scaled(h_adjs[b], w_adj, b, "v")
+            u = work.tile([P, N], F32, name="u")
+            nc.vector.scalar_tensor_tensor(
+                u[:], h_filts[b][:], w_filt[:, b : b + 1], owns[b][:], MULT, ADD
+            )
+            place(b, u, v)
+
+        u_sums = []
+        for b in range(BY_VECTOR, NB):
+            filtered = scaled(h_filts[b], w_filt, b, "filtered")
+            u_sum = psum.tile([P, N], F32, name="u_sum", tag="bank")
+            nc.tensor.matmul(u_sum[:], identity_f32[:], owns[b][:], start=True, stop=False)
+            nc.tensor.matmul(u_sum[:], identity_f32[:], filtered[:], start=False, stop=True)
+            u_sums.append(u_sum)
+        for b in range(BY_VECTOR, NB):
+            v = scaled(h_adjs[b], w_adj, b, "v")
+            u = work.tile([P, N], F32, name="u")
+            nc.scalar.copy(u[:], u_sums[b - BY_VECTOR][:])
+            place(b, u, v)

@@ -8,7 +8,7 @@ NK = N // P
 
 PSUM_BANKS = 8
 
-WARM_UP_MATMULS = 16
+WARM_UP_MATMULS = 13
 BY_VECTOR = 2
 
 FLOPS = 2 * 2 * C * N * N
@@ -47,41 +47,44 @@ def tile_eigenvaluesegmentprec_kernel(
         identity_f32 = held.tile([P, P], F32, name="identity_f32")
         make_identity(nc, identity_f32[:])
 
-        h_rows = held.tile([P, NB, N], BF16, name="h_rows")
-        nc.sync.dma_start(h_rows[:], h_blocks)
-        w_id = held.tile([P, NB], F32, name="w_id")
-        nc.sync.dma_start(w_id[:], cw_id.rearrange("(p b) o -> p (b o)", b=NB))
+        h_first = held.tile([P, 1, N], BF16, name="h_first")
+        nc.sync.dma_start(h_first[:], h_blocks[:, 0:1, :])
+        h_rest = held.tile([P, NB - 1, N], BF16, name="h_rest")
+        nc.sync.dma_start(h_rest[:], h_blocks[:, 1:NB, :])
+        h_rows = [h_first[:, 0, :]] + [h_rest[:, b, :] for b in range(NB - 1)]
 
-        adj = held.tile([P, NK, N], BF16, name="adj")
-        nc.sync.dma_start(adj[:], adj_t.rearrange("(k p) j -> p k j", p=P))
         filt = held.tile([P, NK, N], BF16, name="filt")
         nc.sync.dma_start(filt[:], filt_t.rearrange("(k p) j -> p k j", p=P))
+        adj = held.tile([P, NK, N], BF16, name="adj")
+        nc.sync.dma_start(adj[:], adj_t.rearrange("(k p) j -> p k j", p=P))
 
+        w_id = held.tile([P, NB], F32, name="w_id")
         w_filt = held.tile([P, NB], F32, name="w_filt")
         w_adj = held.tile([P, NB], F32, name="w_adj")
+        nc.sync.dma_start(w_id[:], cw_id.rearrange("(p b) o -> p (b o)", b=NB))
         nc.sync.dma_start(w_filt[:], cw_filt.rearrange("(p b) o -> p (b o)", b=NB))
         nc.sync.dma_start(w_adj[:], cw_adj.rearrange("(p b) o -> p (b o)", b=NB))
 
+        windows = [held.tile([P, S], F32, name=f"window{b}") for b in range(NB)]
+        nc.sync.dma_start(windows[0][:], base_blocks[:, 0, :])
         offsets = held.tile([P, N // 16], U16, name="offsets")
         nc.sync.dma_start(offsets[:], offs)
-
-        windows = [held.tile([P, S], F32, name=f"window{b}") for b in range(NB)]
-        for b in range(NB):
+        for b in range(1, NB):
             nc.sync.dma_start(windows[b][:], base_blocks[:, b, :])
 
-        def flipped(b):
+        def flipped(b, copy):
             h_flip_psum = psum.tile([P, NK, P], BF16, name="h_flip_psum", tag="bank")
             for k in range(NK):
                 nc.tensor.transpose(
-                    h_flip_psum[:, k, :], h_rows[:, b, k * P : (k + 1) * P], identity[:]
+                    h_flip_psum[:, k, :], h_rows[b][:, k * P : (k + 1) * P], identity[:]
                 )
             h_flip = work.tile([P, NK, P], BF16, name="h_flip")
-            nc.vector.tensor_copy(h_flip[:], h_flip_psum[:])
+            copy(h_flip[:], h_flip_psum[:])
             return h_flip
 
         def own_term(b):
             own = work.tile([P, N], F32, name="own")
-            nc.scalar.activation(own[:], h_rows[:, b, :], COPY, scale=w_id[:, b : b + 1])
+            nc.scalar.activation(own[:], h_rows[b], COPY, scale=w_id[:, b : b + 1])
             return own
 
         def product(h_flip, basis, name):
@@ -102,21 +105,30 @@ def tile_eigenvaluesegmentprec_kernel(
             nc.vector.tensor_tensor(windows[b][:].indirect(offsets[:]), u[:], v[:], ADD)
             nc.sync.dma_start(out_blocks[:, b, :], windows[b][:])
 
-        h_flips = [flipped(b) for b in range(NB)]
-        owns = [own_term(b) for b in range(NB)]
-
-        h_adjs, h_filts = [], []
-        for b in range(NB):
-            h_adjs.append(product(h_flips[b], adj, "h_adj"))
-            h_filts.append(product(h_flips[b], filt, "h_filt"))
-
-        for b in range(BY_VECTOR):
-            v = scaled(h_adjs[b], w_adj, b, "v")
+        def weighted_sum(b, h_filt, own):
             u = work.tile([P, N], F32, name="u")
             nc.vector.scalar_tensor_tensor(
-                u[:], h_filts[b][:], w_filt[:, b : b + 1], owns[b][:], MULT, ADD
+                u[:], h_filt[:], w_filt[:, b : b + 1], own[:], MULT, ADD
             )
-            place(b, u, v)
+            return u
+
+        h_flips = [flipped(b, nc.vector.tensor_copy) for b in range(BY_VECTOR)]
+        owns = [own_term(b) for b in range(BY_VECTOR)]
+        h_filts = [product(h_flips[0], filt, "h_filt")]
+        h_adjs = [product(h_flips[0], adj, "h_adj")]
+        h_filts.append(product(h_flips[1], filt, "h_filt"))
+
+        v = scaled(h_adjs[0], w_adj, 0, "v")
+        us = [weighted_sum(b, h_filts[b], owns[b]) for b in range(BY_VECTOR)]
+        place(0, us[0], v)
+
+        h_flips += [flipped(b, nc.scalar.copy) for b in range(BY_VECTOR, NB)]
+        owns += [own_term(b) for b in range(BY_VECTOR, NB)]
+        h_adjs.append(product(h_flips[1], adj, "h_adj"))
+        for b in range(BY_VECTOR, NB):
+            h_filts.append(product(h_flips[b], filt, "h_filt"))
+            h_adjs.append(product(h_flips[b], adj, "h_adj"))
+        place(1, us[1], scaled(h_adjs[1], w_adj, 1, "v"))
 
         u_sums = []
         for b in range(BY_VECTOR, NB):

@@ -72,14 +72,16 @@ def tile_eigenvaluesegmentprec_kernel(
         for b in range(1, NB):
             nc.sync.dma_start(windows[b][:], base_blocks[:, b, :])
 
-        def flipped(b, copy):
-            h_flip_psum = psum.tile([P, NK, P], BF16, name="h_flip_psum", tag="bank")
-            for k in range(NK):
+        def flipped(b, copies):
+            h_flip = []
+            for k, copy in enumerate(copies):
+                half_psum = psum.tile([P, P], BF16, name="half_psum", tag="bank")
                 nc.tensor.transpose(
-                    h_flip_psum[:, k, :], h_rows[b][:, k * P : (k + 1) * P], identity[:]
+                    half_psum[:], h_rows[b][:, k * P : (k + 1) * P], identity[:]
                 )
-            h_flip = work.tile([P, NK, P], BF16, name="h_flip")
-            copy(h_flip[:], h_flip_psum[:])
+                half = work.tile([P, P], BF16, name=f"half{k}")
+                copy(half[:], half_psum[:])
+                h_flip.append(half)
             return h_flip
 
         def own_term(b):
@@ -91,7 +93,7 @@ def tile_eigenvaluesegmentprec_kernel(
             h_basis = psum.tile([P, N], F32, name=name, tag="bank")
             for k in range(NK):
                 nc.tensor.matmul(
-                    h_basis[:], h_flip[:, k, :], basis[:, k, :],
+                    h_basis[:], h_flip[k][:], basis[:, k, :],
                     start=(k == 0), stop=(k == NK - 1),
                 )
             return h_basis
@@ -112,17 +114,19 @@ def tile_eigenvaluesegmentprec_kernel(
             )
             return u
 
-        h_flips = [flipped(b, nc.vector.tensor_copy) for b in range(BY_VECTOR)]
+        h_flips = [flipped(b, NK * [nc.vector.tensor_copy]) for b in range(BY_VECTOR)]
         owns = [own_term(b) for b in range(BY_VECTOR)]
         h_filts = [product(h_flips[0], filt, "h_filt")]
         h_adjs = [product(h_flips[0], adj, "h_adj")]
         h_filts.append(product(h_flips[1], filt, "h_filt"))
 
-        v = scaled(h_adjs[0], w_adj, 0, "v")
-        us = [weighted_sum(b, h_filts[b], owns[b]) for b in range(BY_VECTOR)]
+        us = [weighted_sum(0, h_filts[0], owns[0])]
+        v = work.tile([P, N], F32, name="v")
+        nc.vector.tensor_scalar_mul(v[:], h_adjs[0][:], w_adj[:, 0:1])
+        us.append(weighted_sum(1, h_filts[1], owns[1]))
         place(0, us[0], v)
 
-        h_flips += [flipped(b, nc.scalar.copy) for b in range(BY_VECTOR, NB)]
+        h_flips += [flipped(b, NK * [nc.scalar.copy]) for b in range(BY_VECTOR, NB)]
         owns += [own_term(b) for b in range(BY_VECTOR, NB)]
         h_adjs.append(product(h_flips[1], adj, "h_adj"))
         for b in range(BY_VECTOR, NB):

@@ -39,6 +39,13 @@ def tile_eigenvaluesegmentprec_kernel(
         for _ in range(WARM_UP_MATMULS):
             nc.tensor.matmul(unused[:], zeros[:], zeros[:], start=True, stop=True)
 
+        w_id = held.tile([P, NB], F32, name="w_id")
+        w_filt = held.tile([P, NB], F32, name="w_filt")
+        w_adj = held.tile([P, NB], F32, name="w_adj")
+        nc.scalar.dma_start(w_id[:], cw_id.rearrange("(p b) o -> p (b o)", b=NB))
+        nc.scalar.dma_start(w_filt[:], cw_filt.rearrange("(p b) o -> p (b o)", b=NB))
+        nc.scalar.dma_start(w_adj[:], cw_adj.rearrange("(p b) o -> p (b o)", b=NB))
+
         primed = held.tile([P, 1], F32, name="primed")
         nc.scalar.activation(primed[:], zeros[:, 0:1], COPY)
 
@@ -57,13 +64,6 @@ def tile_eigenvaluesegmentprec_kernel(
         nc.sync.dma_start(filt[:], filt_t.rearrange("(k p) j -> p k j", p=P))
         adj = held.tile([P, NK, N], BF16, name="adj")
         nc.sync.dma_start(adj[:], adj_t.rearrange("(k p) j -> p k j", p=P))
-
-        w_id = held.tile([P, NB], F32, name="w_id")
-        w_filt = held.tile([P, NB], F32, name="w_filt")
-        w_adj = held.tile([P, NB], F32, name="w_adj")
-        nc.sync.dma_start(w_id[:], cw_id.rearrange("(p b) o -> p (b o)", b=NB))
-        nc.sync.dma_start(w_filt[:], cw_filt.rearrange("(p b) o -> p (b o)", b=NB))
-        nc.sync.dma_start(w_adj[:], cw_adj.rearrange("(p b) o -> p (b o)", b=NB))
 
         windows = [held.tile([P, S], F32, name=f"window{b}") for b in range(NB)]
         nc.sync.dma_start(windows[0][:], base_blocks[:, 0, :])
@@ -86,7 +86,11 @@ def tile_eigenvaluesegmentprec_kernel(
 
         def own_term(b):
             own = work.tile([P, N], F32, name="own")
-            nc.scalar.activation(own[:], h_rows[b], COPY, scale=w_id[:, b : b + 1])
+            weight = w_id[:, b : b + 1]
+            if b == 0:
+                nc.vector.tensor_scalar_mul(own[:], h_rows[b], weight)
+            else:
+                nc.scalar.activation(own[:], h_rows[b], COPY, scale=weight)
             return own
 
         def product(h_flip, basis, name):

@@ -8,8 +8,9 @@ NK = N // P
 
 PSUM_BANKS = 8
 
-WARM_UP_MATMULS = 13
-BY_VECTOR = 2
+WARM_UP_MATMULS = 10
+HALF = NB // 2
+BY_VECTOR = HALF
 
 FLOPS = 2 * 2 * C * N * N
 
@@ -54,16 +55,16 @@ def tile_eigenvaluesegmentprec_kernel(
         identity_f32 = held.tile([P, P], F32, name="identity_f32")
         make_identity(nc, identity_f32[:])
 
-        h_first = held.tile([P, 1, N], BF16, name="h_first")
-        nc.sync.dma_start(h_first[:], h_blocks[:, 0:1, :])
-        h_rest = held.tile([P, NB - 1, N], BF16, name="h_rest")
-        nc.sync.dma_start(h_rest[:], h_blocks[:, 1:NB, :])
-        h_rows = [h_first[:, 0, :]] + [h_rest[:, b, :] for b in range(NB - 1)]
+        h_halves = [held.tile([P, HALF, N], BF16, name=f"h_half{i}") for i in range(2)]
+        h_rows = [h_half[:, b, :] for h_half in h_halves for b in range(HALF)]
+        nc.sync.dma_start(h_halves[0][:], h_blocks[:, 0:HALF, :])
 
         filt = held.tile([P, NK, N], BF16, name="filt")
         nc.sync.dma_start(filt[:], filt_t.rearrange("(k p) j -> p k j", p=P))
         adj = held.tile([P, NK, N], BF16, name="adj")
         nc.sync.dma_start(adj[:], adj_t.rearrange("(k p) j -> p k j", p=P))
+
+        nc.sync.dma_start(h_halves[1][:], h_blocks[:, HALF:NB, :])
 
         windows = [held.tile([P, S], F32, name=f"window{b}") for b in range(NB)]
         nc.sync.dma_start(windows[0][:], base_blocks[:, 0, :])
@@ -87,7 +88,7 @@ def tile_eigenvaluesegmentprec_kernel(
         def own_term(b):
             own = work.tile([P, N], F32, name="own")
             weight = w_id[:, b : b + 1]
-            if b == 0:
+            if b < HALF:
                 nc.vector.tensor_scalar_mul(own[:], h_rows[b], weight)
             else:
                 nc.scalar.activation(own[:], h_rows[b], COPY, scale=weight)

@@ -40,13 +40,6 @@ def tile_eigenvaluesegmentprec_kernel(
         for _ in range(WARM_UP_MATMULS):
             nc.tensor.matmul(unused[:], zeros[:], zeros[:], start=True, stop=True)
 
-        w_id = held.tile([P, NB], F32, name="w_id")
-        w_filt = held.tile([P, NB], F32, name="w_filt")
-        w_adj = held.tile([P, NB], F32, name="w_adj")
-        nc.scalar.dma_start(w_id[:], cw_id.rearrange("(p b) o -> p (b o)", b=NB))
-        nc.scalar.dma_start(w_filt[:], cw_filt.rearrange("(p b) o -> p (b o)", b=NB))
-        nc.scalar.dma_start(w_adj[:], cw_adj.rearrange("(p b) o -> p (b o)", b=NB))
-
         primed = held.tile([P, 1], F32, name="primed")
         nc.scalar.activation(primed[:], zeros[:, 0:1], COPY)
 
@@ -58,6 +51,13 @@ def tile_eigenvaluesegmentprec_kernel(
         h_halves = [held.tile([P, HALF, N], BF16, name=f"h_half{i}") for i in range(2)]
         h_rows = [h_half[:, b, :] for h_half in h_halves for b in range(HALF)]
         nc.sync.dma_start(h_halves[0][:], h_blocks[:, 0:HALF, :])
+
+        w_id = held.tile([P, NB], F32, name="w_id")
+        w_filt = held.tile([P, NB], F32, name="w_filt")
+        w_adj = held.tile([P, NB], F32, name="w_adj")
+        nc.sync.dma_start(w_id[:], cw_id.rearrange("(p b) o -> p (b o)", b=NB))
+        nc.sync.dma_start(w_filt[:], cw_filt.rearrange("(p b) o -> p (b o)", b=NB))
+        nc.sync.dma_start(w_adj[:], cw_adj.rearrange("(p b) o -> p (b o)", b=NB))
 
         filt = held.tile([P, NK, N], BF16, name="filt")
         nc.sync.dma_start(filt[:], filt_t.rearrange("(k p) j -> p k j", p=P))
@@ -122,32 +122,28 @@ def tile_eigenvaluesegmentprec_kernel(
         h_flips = [flipped(b, NK * [nc.vector.tensor_copy]) for b in range(BY_VECTOR)]
         owns = [own_term(b) for b in range(BY_VECTOR)]
         h_filts = [product(h_flips[0], filt, "h_filt")]
-        h_adjs = [product(h_flips[0], adj, "h_adj")]
+        h_adj = product(h_flips[0], adj, "h_adj")
         h_filts.append(product(h_flips[1], filt, "h_filt"))
 
         us = [weighted_sum(0, h_filts[0], owns[0])]
         v = work.tile([P, N], F32, name="v")
-        nc.vector.tensor_scalar_mul(v[:], h_adjs[0][:], w_adj[:, 0:1])
+        nc.vector.tensor_scalar_mul(v[:], h_adj[:], w_adj[:, 0:1])
         us.append(weighted_sum(1, h_filts[1], owns[1]))
         place(0, us[0], v)
 
         h_flips += [flipped(b, NK * [nc.scalar.copy]) for b in range(BY_VECTOR, NB)]
         owns += [own_term(b) for b in range(BY_VECTOR, NB)]
-        h_adjs.append(product(h_flips[1], adj, "h_adj"))
-        for b in range(BY_VECTOR, NB):
-            h_filts.append(product(h_flips[b], filt, "h_filt"))
-            h_adjs.append(product(h_flips[b], adj, "h_adj"))
-        place(1, us[1], scaled(h_adjs[1], w_adj, 1, "v"))
+        h_adj = product(h_flips[1], adj, "h_adj")
+        place(1, us[1], scaled(h_adj, w_adj, 1, "v"))
 
-        u_sums = []
         for b in range(BY_VECTOR, NB):
-            filtered = scaled(h_filts[b], w_filt, b, "filtered")
+            h_filt = product(h_flips[b], filt, "h_filt")
             u_sum = psum.tile([P, N], F32, name="u_sum", tag="bank")
             nc.tensor.matmul(u_sum[:], identity_f32[:], owns[b][:], start=True, stop=False)
+            h_adj = product(h_flips[b], adj, "h_adj")
+            filtered = scaled(h_filt, w_filt, b, "filtered")
             nc.tensor.matmul(u_sum[:], identity_f32[:], filtered[:], start=False, stop=True)
-            u_sums.append(u_sum)
-        for b in range(BY_VECTOR, NB):
-            v = scaled(h_adjs[b], w_adj, b, "v")
+            v = scaled(h_adj, w_adj, b, "v")
             u = work.tile([P, N], F32, name="u")
-            nc.scalar.copy(u[:], u_sums[b - BY_VECTOR][:])
+            nc.scalar.copy(u[:], u_sum[:])
             place(b, u, v)

@@ -53,16 +53,15 @@ def tile_eigenvaluesegmentprec_kernel(
         nc.sync.dma_start(h_halves[0][:], h_blocks[:, 0:HALF, :])
 
         w_id = held.tile([P, NB], F32, name="w_id")
-        w_filt = held.tile([P, NB], F32, name="w_filt")
-        w_adj = held.tile([P, NB], F32, name="w_adj")
         nc.sync.dma_start(w_id[:], cw_id.rearrange("(p b) o -> p (b o)", b=NB))
-        nc.sync.dma_start(w_filt[:], cw_filt.rearrange("(p b) o -> p (b o)", b=NB))
-        nc.sync.dma_start(w_adj[:], cw_adj.rearrange("(p b) o -> p (b o)", b=NB))
-
         filt = held.tile([P, NK, N], BF16, name="filt")
-        nc.sync.dma_start(filt[:], filt_t.rearrange("(k p) j -> p k j", p=P))
+        nc.sync.dma_start(filt[:], filt_t.rearrange("(p k) j -> p k j", k=NK))
+        w_filt = held.tile([P, NB], F32, name="w_filt")
+        nc.sync.dma_start(w_filt[:], cw_filt.rearrange("(p b) o -> p (b o)", b=NB))
         adj = held.tile([P, NK, N], BF16, name="adj")
-        nc.sync.dma_start(adj[:], adj_t.rearrange("(k p) j -> p k j", p=P))
+        nc.sync.dma_start(adj[:], adj_t.rearrange("(p k) j -> p k j", k=NK))
+        w_adj = held.tile([P, NB], F32, name="w_adj")
+        nc.sync.dma_start(w_adj[:], cw_adj.rearrange("(p b) o -> p (b o)", b=NB))
 
         nc.sync.dma_start(h_halves[1][:], h_blocks[:, HALF:NB, :])
 
@@ -78,7 +77,7 @@ def tile_eigenvaluesegmentprec_kernel(
             for k, copy in enumerate(copies):
                 half_psum = psum.tile([P, P], BF16, name="half_psum", tag="bank")
                 nc.tensor.transpose(
-                    half_psum[:], h_rows[b][:, k * P : (k + 1) * P], identity[:]
+                    half_psum[:], h_rows[b][:, k::NK], identity[:]
                 )
                 half = work.tile([P, P], BF16, name=f"half{k}")
                 copy(half[:], half_psum[:])

import concourse.mybir as mybir
from concourse.masks import make_identity

P = 128
C, S, N = 512, 512, 256
NB = C // P
NK = N // P

PSUM_BANKS = 8

WARM_UP_MATMULS = 10
HALF = NB // 2
BY_VECTOR = HALF

FLOPS = 2 * 2 * C * N * N

BF16, F32, U16 = mybir.dt.bfloat16, mybir.dt.float32, mybir.dt.uint16
MULT, ADD = mybir.AluOpType.mult, mybir.AluOpType.add
COPY = mybir.ActivationFunctionType.Copy


def tile_eigenvaluesegmentprec_kernel(
    tc, base, h, filt_t, adj_t, cw_filt, cw_id, cw_adj, offs, out
):
    nc = tc.nc

    h_blocks = h.rearrange("(p b) i -> p b i", b=NB)
    base_blocks = base.rearrange("(p b) s -> p b s", b=NB)
    out_blocks = out.rearrange("(p b) s -> p b s", b=NB)

    with (
        tc.tile_pool(name="held", bufs=1) as held,
        tc.tile_pool(name="work", bufs=NB) as work,
        tc.psum_pool(name="idle", bufs=1) as idle,
        tc.psum_pool(name="psum", bufs=PSUM_BANKS - 1) as psum,
    ):
        zeros = held.tile([P, P], BF16, name="zeros")
        nc.gpsimd.memset(zeros[:], 0.0)
        unused = idle.tile([P, P], F32, name="unused")
        for _ in range(WARM_UP_MATMULS):
            nc.tensor.matmul(unused[:], zeros[:], zeros[:], start=True, stop=True)

        primed = held.tile([P, 1], F32, name="primed")
        nc.scalar.activation(primed[:], zeros[:, 0:1], COPY)

        identity = held.tile([P, P], BF16, name="identity")
        make_identity(nc, identity[:])
        identity_f32 = held.tile([P, P], F32, name="identity_f32")
        make_identity(nc, identity_f32[:])

        h_halves = [held.tile([P, HALF, N], BF16, name=f"h_half{i}") for i in range(2)]
        h_rows = [h_half[:, b, :] for h_half in h_halves for b in range(HALF)]
        nc.sync.dma_start(h_halves[0][:], h_blocks[:, 0:HALF, :])

        w_id = held.tile([P, NB], F32, name="w_id")
        nc.sync.dma_start(w_id[:], cw_id.rearrange("(p b) o -> p (b o)", b=NB))
        filt = held.tile([P, NK, N], BF16, name="filt")
        nc.sync.dma_start(filt[:], filt_t.rearrange("(p k) j -> p k j", k=NK))
        w_filt = held.tile([P, NB], F32, name="w_filt")
        nc.sync.dma_start(w_filt[:], cw_filt.rearrange("(p b) o -> p (b o)", b=NB))
        adj = held.tile([P, NK, N], BF16, name="adj")
        nc.sync.dma_start(adj[:], adj_t.rearrange("(p k) j -> p k j", k=NK))
        w_adj = held.tile([P, NB], F32, name="w_adj")
        nc.sync.dma_start(w_adj[:], cw_adj.rearrange("(p b) o -> p (b o)", b=NB))

        nc.sync.dma_start(h_halves[1][:], h_blocks[:, HALF:NB, :])

        windows = [held.tile([P, S], F32, name=f"window{b}") for b in range(NB)]
        nc.sync.dma_start(windows[0][:], base_blocks[:, 0, :])
        offsets = held.tile([P, N // 16], U16, name="offsets")
        nc.sync.dma_start(offsets[:], offs)
        for b in range(1, NB):
            nc.sync.dma_start(windows[b][:], base_blocks[:, b, :])

        def flipped(b, copies):
            h_flip = []
            for k, copy in enumerate(copies):
                half_psum = psum.tile([P, P], BF16, name="half_psum", tag="bank")
                nc.tensor.transpose(
                    half_psum[:], h_rows[b][:, k::NK], identity[:]
                )
                half = work.tile([P, P], BF16, name=f"half{k}")
                copy(half[:], half_psum[:])
                h_flip.append(half)
            return h_flip

        def own_term(b):
            own = work.tile([P, N], F32, name="own")
            weight = w_id[:, b : b + 1]
            if b < HALF:
                nc.vector.tensor_scalar_mul(own[:], h_rows[b], weight)
            else:
                nc.scalar.activation(own[:], h_rows[b], COPY, scale=weight)
            return own

        def product(h_flip, basis, name):
            h_basis = psum.tile([P, N], F32, name=name, tag="bank")
            for k in range(NK):
                nc.tensor.matmul(
                    h_basis[:], h_flip[k][:], basis[:, k, :],
                    start=(k == 0), stop=(k == NK - 1),
                )
            return h_basis

        def scaled(h_basis, weights, b, name):
            term = work.tile([P, N], F32, name=name)
            nc.scalar.activation(term[:], h_basis[:], COPY, scale=weights[:, b : b + 1])
            return term

        def place(b, u, v):
            nc.vector.tensor_tensor(windows[b][:].indirect(offsets[:]), u[:], v[:], ADD)
            nc.sync.dma_start(out_blocks[:, b, :], windows[b][:])

        def weighted_sum(b, h_filt, own):
            u = work.tile([P, N], F32, name="u")
            nc.vector.scalar_tensor_tensor(
                u[:], h_filt[:], w_filt[:, b : b + 1], own[:], MULT, ADD
            )
            return u

        h_flips = [flipped(b, NK * [nc.vector.tensor_copy]) for b in range(BY_VECTOR)]
        owns = [own_term(b) for b in range(BY_VECTOR)]
        h_filts = [product(h_flips[0], filt, "h_filt")]
        h_adj = product(h_flips[0], adj, "h_adj")
        h_filts.append(product(h_flips[1], filt, "h_filt"))

        us = [weighted_sum(0, h_filts[0], owns[0])]
        v = work.tile([P, N], F32, name="v")
        nc.vector.tensor_scalar_mul(v[:], h_adj[:], w_adj[:, 0:1])
        us.append(weighted_sum(1, h_filts[1], owns[1]))
        place(0, us[0], v)

        h_flips += [flipped(b, NK * [nc.scalar.copy]) for b in range(BY_VECTOR, NB)]
        owns += [own_term(b) for b in range(BY_VECTOR, NB)]
        h_adj = product(h_flips[1], adj, "h_adj")
        place(1, us[1], scaled(h_adj, w_adj, 1, "v"))

        for b in range(BY_VECTOR, NB):
            h_filt = product(h_flips[b], filt, "h_filt")
            u_sum = psum.tile([P, N], F32, name="u_sum", tag="bank")
            nc.tensor.matmul(u_sum[:], identity_f32[:], owns[b][:], start=True, stop=False)
            h_adj = product(h_flips[b], adj, "h_adj")
            filtered = scaled(h_filt, w_filt, b, "filtered")
            nc.tensor.matmul(u_sum[:], identity_f32[:], filtered[:], start=False, stop=True)
            v = scaled(h_adj, w_adj, b, "v")
            u = work.tile([P, N], F32, name="u")
            nc.scalar.copy(u[:], u_sum[:])
            place(b, u, v)
